import numpy as np
import ml_dtypes


def mxq(x, axis, fmt="e4m3"):
    dtype, down = {"e4m3": (ml_dtypes.float8_e4m3fn, 7), "e5m2": (ml_dtypes.float8_e5m2, 14)}[fmt]
    v = np.moveaxis(np.asarray(x, np.float32).astype(ml_dtypes.bfloat16).astype(np.float64), axis, -1)
    blocks = v.reshape(v.shape[:-1] + (-1, 32))
    amax = np.abs(blocks).max(-1, keepdims=True)
    byte = np.maximum(np.where(amax > 0, np.frexp(amax)[1] - 1 + 127, 0) - down, 1)
    scale = np.exp2(byte - 127.0)
    codes = (blocks / scale).astype(np.float32).astype(dtype).astype(np.float64)
    return np.moveaxis((codes * scale).reshape(v.shape), -1, axis)


WIDE = False


def mx_kscale(k):
    if not WIDE:
        return np.ones(k)
    levels = np.array([20, -20, 10, -10, 0])
    a = np.random.permutation(np.resize(levels, k // 512 * 4)).reshape(k // 512, 4)
    idx = np.arange(k)
    return np.exp2(a[idx // 512, idx % 128 // 32])


BF16 = ml_dtypes.bfloat16


def bf(x):
    return np.asarray(x, np.float32).astype(BF16)


def f64(x):
    return np.asarray(x).astype(np.float64)


B, Nb1, Nw1, Nb2x, Nb2y, Nw2x, Nw2y, R, C = 512, 2, 16, 1, 1, 128, 64, 128, 2
J1 = Nb1 * Nb1
J3 = Nb2x * Nb2y
J2 = J3 * J1
K3 = J1 * R
L3 = C * Nw2x * Nw2y


def to_grid(y):
    y = y.reshape(B, Nb2x, Nb2y, Nw2x, Nw2y, C).transpose(0, 1, 3, 2, 4, 5)
    return y.reshape(B, Nb2x * Nw2x, Nb2y * Nw2y, C)


def from_grid(g):
    g = g.reshape(B, Nb2x, Nw2x, Nb2y, Nw2y, C).transpose(0, 1, 3, 2, 4, 5)
    return g.reshape(B, J3, L3)


def setup_inputs():
    u = mx_kscale(L3)
    h_switch = np.random.standard_normal((B, J2, R))
    k2 = np.random.standard_normal((J2, R, R)) / np.sqrt(R)
    b2 = np.random.standard_normal((1, J2, R)) * 0.3
    k3 = np.random.standard_normal((J3, K3, L3)) / np.sqrt(K3) / u[None, None, :]
    b3 = np.random.standard_normal((1, J3, L3)) * 0.3
    g = np.random.standard_normal((B, J3, L3)) * np.exp2(np.random.randint(-12, 1, (B, 1, 1))) * 4.0 * u[None, None, :]
    return {"h_switch": bf(h_switch), "k2": bf(k2), "b2": bf(b2), "k3": bf(k3), "b3": bf(b3),
            "grad_out": bf(to_grid(g))}


def reference(h_switch, k2, b2, k3, b3, grad_out):
    dy = from_grid(f64(grad_out))
    dyq = mxq(dy, 2, "e5m2").transpose(1, 0, 2)
    k3q = mxq(f64(k3), 2, "e4m3").transpose(0, 2, 1)
    dg = (dyq @ k3q).transpose(1, 0, 2)
    dg = dg.reshape(B, J2, R)
    dh = dg.transpose(1, 0, 2) @ f64(k2).transpose(0, 2, 1)
    return dh.transpose(1, 0, 2)

@@ -1,0 +1,188 @@
+from contextlib import ExitStack
+
+import concourse.mybir as mybir
+from concourse.masks import make_identity
+
+F32 = mybir.dt.float32
+BF16 = mybir.dt.bfloat16
+U32 = mybir.dt.uint32
+U8 = mybir.dt.uint8
+E4M3_X4 = mybir.dt.float8_e4m3fn_x4
+E5M2_X4 = mybir.dt.float8_e5m2_x4
+
+P = 128
+ROWS = 512
+ROW_TILES = ROWS // P
+WINDOW = 16384
+GROUPS = 4
+R = 128
+K_PASS = 4 * P
+PASSES = WINDOW // K_PASS
+WORDS = K_PASS // 2
+BANK = 512
+
+CHUNK_PASSES = 2
+CHUNKS = PASSES // CHUNK_PASSES
+PREFETCH = 3
+RUN_PASSES = 1
+RUNS = PASSES // RUN_PASSES
+LAG_RUNS = 1
+
+FLOPS = 2 * ROWS * ROWS * WINDOW + 2 * ROWS * GROUPS * R * R
+
+
+def transpose_pass(nc, banks, ident, raw, local_pass, grouped, vector_helps):
+    raw_words = raw[:].bitcast(F32)
+    grouped_words = grouped[:].bitcast(F32)
+    first_word = local_pass * WORDS
+    tiles_per_bank = BANK // (2 * P)
+    for half in range(ROW_TILES // tiles_per_bank):
+        bank = banks.tile([P, 2, tiles_per_bank * P], F32, tag="bank")
+        for u in range(2):
+            for i in range(tiles_per_bank):
+                nc.tensor.transpose(
+                    bank[:, u, i * P : (i + 1) * P],
+                    raw_words[
+                        :,
+                        half * tiles_per_bank + i,
+                        first_word + u * P : first_word + (u + 1) * P,
+                    ],
+                    ident[:],
+                )
+        src = bank[:].rearrange("p u c -> p c u")
+        dst = grouped_words[:, half * BANK : (half + 1) * BANK].rearrange(
+            "p (c u) -> p c u", u=2
+        )
+        if vector_helps and half == 1:
+            nc.vector.tensor_copy(out=dst, in_=src)
+        else:
+            nc.scalar.copy(out=dst, in_=src)
+
+
+def tile_switchnet_fstar_pb_k_kernel(tc, h_switch, k2, b2, k3, b3, grad_out, out):
+    nc = tc.nc
+    dy_rows = grad_out.rearrange("(t p) x y c -> p t (x y c)", p=P)
+    k3_rows = k3[0].rearrange("(t p) l -> p t l", p=P)
+    out_rows = out.rearrange("(t p) j r -> t p (j r)", p=P)
+
+    with ExitStack() as ctx:
+        const = ctx.enter_context(tc.tile_pool(name="const", bufs=1))
+        raw_pool = ctx.enter_context(tc.tile_pool(name="raw", bufs=PREFETCH + 1))
+        grouped_pool = ctx.enter_context(tc.tile_pool(name="grouped", bufs=2 * RUN_PASSES))
+        mx_pool = ctx.enter_context(
+            tc.tile_pool(name="mx", bufs=(LAG_RUNS + 2) * RUN_PASSES)
+        )
+        result_pool = ctx.enter_context(tc.tile_pool(name="result", bufs=ROW_TILES))
+        acc_pool = ctx.enter_context(tc.psum_pool(name="acc", bufs=1))
+        banks = ctx.enter_context(tc.psum_pool(name="banks", bufs=4))
+
+        ident = const.tile([P, P], F32)
+        make_identity(nc, ident[:])
+
+        ctx.enter_context(tc.manual_schedule())
+
+        def load_chunk(c):
+            k_cols = slice(c * CHUNK_PASSES * K_PASS, (c + 1) * CHUNK_PASSES * K_PASS)
+            dy_raw = raw_pool.tile([P, ROW_TILES, CHUNK_PASSES * K_PASS], BF16)
+            nc.sync.dma_start(out=dy_raw[:], in_=dy_rows[:, :, k_cols])
+            k3_raw = raw_pool.tile([P, ROW_TILES, CHUNK_PASSES * K_PASS], BF16)
+            nc.sync.dma_start(out=k3_raw[:], in_=k3_rows[:, :, k_cols])
+            return dy_raw, k3_raw
+
+        raw = {}
+        for c in range(PREFETCH):
+            raw[c] = load_chunk(c)
+
+        k2_bf16 = const.tile([P, GROUPS, R], BF16)
+        nc.scalar.dma_start(out=k2_bf16[:], in_=k2.rearrange("j r q -> r j q"))
+        k2_f32 = const.tile([P, GROUPS, R], F32)
+        nc.vector.tensor_copy(out=k2_f32[:], in_=k2_bf16[:])
+        k2_bank = banks.tile([P, GROUPS, R], F32, tag="bank")
+        for j in range(GROUPS):
+            nc.tensor.transpose(k2_bank[:, j, :], k2_f32[:, j, :], ident[:])
+        k2_t = const.tile([P, GROUPS, R], F32)
+        nc.scalar.copy(out=k2_t[:], in_=k2_bank[:])
+
+        dg_acc = [
+            acc_pool.tile([P, ROWS], F32, name="dg_acc%d" % j) for j in range(GROUPS)
+        ]
+
+        quantised = {}
+
+        def multiply_run(run):
+            for g in range(run * RUN_PASSES, (run + 1) * RUN_PASSES):
+                dy_codes, dy_scales, k3_codes, k3_scales = quantised[g]
+                for j in range(GROUPS):
+                    group_cols = slice(j * R, (j + 1) * R)
+                    nc.tensor.matmul_mx(
+                        out=dg_acc[j][:],
+                        lhsT=k3_codes[:, group_cols].bitcast(E4M3_X4),
+                        lhsT_scale=k3_scales[:, group_cols],
+                        rhs=dy_codes[:].bitcast(E5M2_X4),
+                        rhs_scale=dy_scales[:],
+                        start=(g == 0),
+                        stop=(g == PASSES - 1),
+                    )
+
+        for run in range(RUNS):
+            run_passes = range(run * RUN_PASSES, (run + 1) * RUN_PASSES)
+            grouped = {}
+            for g in run_passes:
+                c, local_pass = divmod(g, CHUNK_PASSES)
+                if local_pass == 0 and c + PREFETCH < CHUNKS:
+                    raw[c + PREFETCH] = load_chunk(c + PREFETCH)
+                dy_raw, k3_raw = raw[c]
+                dy_grouped = grouped_pool.tile([P, 4 * ROWS], BF16, align_bytes=64)
+                transpose_pass(nc, banks, ident, dy_raw, local_pass, dy_grouped, True)
+                k3_grouped = grouped_pool.tile([P, 4 * ROWS], BF16, align_bytes=64)
+                transpose_pass(
+                    nc, banks, ident, k3_raw, local_pass, k3_grouped, g != run_passes[-1]
+                )
+                grouped[g] = (dy_grouped, k3_grouped)
+
+            for g in run_passes:
+                dy_grouped, k3_grouped = grouped[g]
+                dy_codes = mx_pool.tile([P, ROWS], U32, align_bytes=64)
+                dy_scales = mx_pool.tile([P, ROWS], U8, align_bytes=64)
+                nc.vector.quantize_mx(
+                    out=dy_codes[:].bitcast(E5M2_X4), scales=dy_scales[:], in_=dy_grouped[:]
+                )
+                k3_codes = mx_pool.tile([P, ROWS], U32, align_bytes=64)
+                k3_scales = mx_pool.tile([P, ROWS], U8, align_bytes=64)
+                nc.vector.quantize_mx(
+                    out=k3_codes[:].bitcast(E4M3_X4), scales=k3_scales[:], in_=k3_grouped[:]
+                )
+                quantised[g] = (dy_codes, dy_scales, k3_codes, k3_scales)
+
+            if run >= LAG_RUNS:
+                multiply_run(run - LAG_RUNS)
+        for run in range(RUNS - LAG_RUNS, RUNS):
+            multiply_run(run)
+
+        dg_t = const.tile([P, GROUPS, ROWS], F32)
+        out_banks = [
+            banks.tile([P, GROUPS, R], F32, tag="bank", name="out_bank%d" % t)
+            for t in range(ROW_TILES)
+        ]
+        for j in range(GROUPS):
+            if j % 2 == 0:
+                nc.scalar.copy(out=dg_t[:, j, :], in_=dg_acc[j][:])
+            else:
+                nc.vector.tensor_copy(out=dg_t[:, j, :], in_=dg_acc[j][:])
+            for t in range(ROW_TILES):
+                nc.tensor.matmul(
+                    out=out_banks[t][:, j, :],
+                    lhsT=dg_t[:, j, t * P : (t + 1) * P],
+                    rhs=k2_t[:, j, :],
+                    start=True,
+                    stop=True,
+                )
+        for t in range(ROW_TILES):
+            result = result_pool.tile([P, GROUPS * R], F32)
+            if t % 2 == 0:
+                nc.scalar.copy(out=result[:], in_=out_banks[t][:].rearrange("p j r -> p (j r)"))
+            else:
+                nc.vector.tensor_copy(
+                    out=result[:], in_=out_banks[t][:].rearrange("p j r -> p (j r)")
+                )
+            nc.sync.dma_start(out=out_rows[t], in_=result[:])

@@ -24,7 +24,7 @@ BANK = 512
 CHUNK_PASSES = 2
 CHUNKS = PASSES // CHUNK_PASSES
 PREFETCH = 3
-RUN_PASSES = 1
+RUN_PASSES = 2
 RUNS = PASSES // RUN_PASSES
 LAG_RUNS = 1
 
@@ -126,22 +126,29 @@ def tile_switchnet_fstar_pb_k_kernel(tc, h_switch, k2, b2, k3, b3, grad_out, out
 
         for run in range(RUNS):
             run_passes = range(run * RUN_PASSES, (run + 1) * RUN_PASSES)
-            grouped = {}
             for g in run_passes:
                 c, local_pass = divmod(g, CHUNK_PASSES)
                 if local_pass == 0 and c + PREFETCH < CHUNKS:
                     raw[c + PREFETCH] = load_chunk(c + PREFETCH)
-                dy_raw, k3_raw = raw[c]
+
+            all_dy_grouped = {}
+            for g in run_passes:
+                c, local_pass = divmod(g, CHUNK_PASSES)
                 dy_grouped = grouped_pool.tile([P, 4 * ROWS], BF16, align_bytes=64)
-                transpose_pass(nc, banks, ident, dy_raw, local_pass, dy_grouped, True)
+                transpose_pass(nc, banks, ident, raw[c][0], local_pass, dy_grouped, True)
+                all_dy_grouped[g] = dy_grouped
+            all_k3_grouped = {}
+            for g in run_passes:
+                c, local_pass = divmod(g, CHUNK_PASSES)
                 k3_grouped = grouped_pool.tile([P, 4 * ROWS], BF16, align_bytes=64)
                 transpose_pass(
-                    nc, banks, ident, k3_raw, local_pass, k3_grouped, g != run_passes[-1]
+                    nc, banks, ident, raw[c][1], local_pass, k3_grouped, g != run_passes[-1]
                 )
-                grouped[g] = (dy_grouped, k3_grouped)
+                all_k3_grouped[g] = k3_grouped
 
             for g in run_passes:
-                dy_grouped, k3_grouped = grouped[g]
+                dy_grouped = all_dy_grouped[g]
+                k3_grouped = all_k3_grouped[g]
                 dy_codes = mx_pool.tile([P, ROWS], U32, align_bytes=64)
                 dy_scales = mx_pool.tile([P, ROWS], U8, align_bytes=64)
                 nc.vector.quantize_mx(

@@ -22,9 +22,10 @@ WORDS = K_PASS // 2
 BANK = 512
 
 CHUNK_PASSES = 2
-CHUNKS = PASSES // CHUNK_PASSES
-PREFETCH = 3
-RUN_PASSES = 2
+CHUNK_WIDTHS = [CHUNK_PASSES // 2] * 2 + [CHUNK_PASSES] * (PASSES // CHUNK_PASSES - 1)
+CHUNKS = len(CHUNK_WIDTHS)
+PREFETCH = 4
+RUN_PASSES = 1
 RUNS = PASSES // RUN_PASSES
 LAG_RUNS = 1
 
@@ -78,30 +79,31 @@ def tile_switchnet_fstar_pb_k_kernel(tc, h_switch, k2, b2, k3, b3, grad_out, out
 
         ident = const.tile([P, P], F32)
         make_identity(nc, ident[:])
+        ident_bf16 = const.tile([P, P], BF16)
+        make_identity(nc, ident_bf16[:])
 
         ctx.enter_context(tc.manual_schedule())
 
+        chunk_of = []
+        for c in range(CHUNKS):
+            chunk_of.extend([(c, local_pass) for local_pass in range(CHUNK_WIDTHS[c])])
+
         def load_chunk(c):
-            k_cols = slice(c * CHUNK_PASSES * K_PASS, (c + 1) * CHUNK_PASSES * K_PASS)
+            first_k = chunk_of.index((c, 0)) * K_PASS
+            width = CHUNK_WIDTHS[c] * K_PASS
             dy_raw = raw_pool.tile([P, ROW_TILES, CHUNK_PASSES * K_PASS], BF16)
-            nc.sync.dma_start(out=dy_raw[:], in_=dy_rows[:, :, k_cols])
+            nc.sync.dma_start(
+                out=dy_raw[:, :, :width], in_=dy_rows[:, :, first_k : first_k + width]
+            )
             k3_raw = raw_pool.tile([P, ROW_TILES, CHUNK_PASSES * K_PASS], BF16)
-            nc.sync.dma_start(out=k3_raw[:], in_=k3_rows[:, :, k_cols])
+            nc.sync.dma_start(
+                out=k3_raw[:, :, :width], in_=k3_rows[:, :, first_k : first_k + width]
+            )
             return dy_raw, k3_raw
 
         raw = {}
         for c in range(PREFETCH):
             raw[c] = load_chunk(c)
-
-        k2_bf16 = const.tile([P, GROUPS, R], BF16)
-        nc.scalar.dma_start(out=k2_bf16[:], in_=k2.rearrange("j r q -> r j q"))
-        k2_f32 = const.tile([P, GROUPS, R], F32)
-        nc.vector.tensor_copy(out=k2_f32[:], in_=k2_bf16[:])
-        k2_bank = banks.tile([P, GROUPS, R], F32, tag="bank")
-        for j in range(GROUPS):
-            nc.tensor.transpose(k2_bank[:, j, :], k2_f32[:, j, :], ident[:])
-        k2_t = const.tile([P, GROUPS, R], F32)
-        nc.scalar.copy(out=k2_t[:], in_=k2_bank[:])
 
         dg_acc = [
             acc_pool.tile([P, ROWS], F32, name="dg_acc%d" % j) for j in range(GROUPS)
@@ -126,29 +128,22 @@ def tile_switchnet_fstar_pb_k_kernel(tc, h_switch, k2, b2, k3, b3, grad_out, out
 
         for run in range(RUNS):
             run_passes = range(run * RUN_PASSES, (run + 1) * RUN_PASSES)
+            grouped = {}
             for g in run_passes:
-                c, local_pass = divmod(g, CHUNK_PASSES)
+                c, local_pass = chunk_of[g]
                 if local_pass == 0 and c + PREFETCH < CHUNKS:
                     raw[c + PREFETCH] = load_chunk(c + PREFETCH)
-
-            all_dy_grouped = {}
-            for g in run_passes:
-                c, local_pass = divmod(g, CHUNK_PASSES)
+                dy_raw, k3_raw = raw[c]
                 dy_grouped = grouped_pool.tile([P, 4 * ROWS], BF16, align_bytes=64)
-                transpose_pass(nc, banks, ident, raw[c][0], local_pass, dy_grouped, True)
-                all_dy_grouped[g] = dy_grouped
-            all_k3_grouped = {}
-            for g in run_passes:
-                c, local_pass = divmod(g, CHUNK_PASSES)
+                transpose_pass(nc, banks, ident, dy_raw, local_pass, dy_grouped, True)
                 k3_grouped = grouped_pool.tile([P, 4 * ROWS], BF16, align_bytes=64)
                 transpose_pass(
-                    nc, banks, ident, raw[c][1], local_pass, k3_grouped, g != run_passes[-1]
+                    nc, banks, ident, k3_raw, local_pass, k3_grouped, g != run_passes[-1]
                 )
-                all_k3_grouped[g] = k3_grouped
+                grouped[g] = (dy_grouped, k3_grouped)
 
             for g in run_passes:
-                dy_grouped = all_dy_grouped[g]
-                k3_grouped = all_k3_grouped[g]
+                dy_grouped, k3_grouped = grouped[g]
                 dy_codes = mx_pool.tile([P, ROWS], U32, align_bytes=64)
                 dy_scales = mx_pool.tile([P, ROWS], U8, align_bytes=64)
                 nc.vector.quantize_mx(
@@ -163,33 +158,38 @@ def tile_switchnet_fstar_pb_k_kernel(tc, h_switch, k2, b2, k3, b3, grad_out, out
 
             if run >= LAG_RUNS:
                 multiply_run(run - LAG_RUNS)
+
+        k2_rows = const.tile([P, GROUPS, R], BF16)
+        nc.sync.dma_start(out=k2_rows[:], in_=k2.rearrange("j r q -> r j q"))
+        k2_bank = banks.tile([P, GROUPS, R], BF16, tag="bank")
+        for j in range(GROUPS):
+            nc.tensor.transpose(k2_bank[:, j, :], k2_rows[:, j, :], ident_bf16[:])
+        k2_t = const.tile([P, GROUPS, R], F32)
+        nc.scalar.copy(out=k2_t[:], in_=k2_bank[:])
+
         for run in range(RUNS - LAG_RUNS, RUNS):
             multiply_run(run)
 
         dg_t = const.tile([P, GROUPS, ROWS], F32)
-        out_banks = [
-            banks.tile([P, GROUPS, R], F32, tag="bank", name="out_bank%d" % t)
-            for t in range(ROW_TILES)
-        ]
         for j in range(GROUPS):
             if j % 2 == 0:
                 nc.scalar.copy(out=dg_t[:, j, :], in_=dg_acc[j][:])
             else:
                 nc.vector.tensor_copy(out=dg_t[:, j, :], in_=dg_acc[j][:])
-            for t in range(ROW_TILES):
+
+        for t in range(ROW_TILES):
+            out_bank = banks.tile([P, GROUPS, R], F32, tag="bank")
+            for j in range(GROUPS):
                 nc.tensor.matmul(
-                    out=out_banks[t][:, j, :],
+                    out=out_bank[:, j, :],
                     lhsT=dg_t[:, j, t * P : (t + 1) * P],
                     rhs=k2_t[:, j, :],
                     start=True,
                     stop=True,
                 )
-        for t in range(ROW_TILES):
-            result = result_pool.tile([P, GROUPS * R], F32)
+            result = result_pool.tile([P, GROUPS, R], F32)
             if t % 2 == 0:
-                nc.scalar.copy(out=result[:], in_=out_banks[t][:].rearrange("p j r -> p (j r)"))
+                nc.scalar.copy(out=result[:], in_=out_bank[:])
             else:
-                nc.vector.tensor_copy(
-                    out=result[:], in_=out_banks[t][:].rearrange("p j r -> p (j r)")
-                )
-            nc.sync.dma_start(out=out_rows[t], in_=result[:])
+                nc.vector.tensor_copy(out=result[:], in_=out_bank[:])
+            nc.sync.dma_start(out=out_rows[t], in_=result[:].rearrange("p j r -> p (j r)"))

@@ -25,9 +25,6 @@ CHUNK_PASSES = 2
 CHUNK_WIDTHS = [CHUNK_PASSES // 2] * 2 + [CHUNK_PASSES] * (PASSES // CHUNK_PASSES - 1)
 CHUNKS = len(CHUNK_WIDTHS)
 PREFETCH = 4
-RUN_PASSES = 1
-RUNS = PASSES // RUN_PASSES
-LAG_RUNS = 1
 
 FLOPS = 2 * ROWS * ROWS * WINDOW + 2 * ROWS * GROUPS * R * R
 
@@ -69,9 +66,9 @@ def tile_switchnet_fstar_pb_k_kernel(tc, h_switch, k2, b2, k3, b3, grad_out, out
     with ExitStack() as ctx:
         const = ctx.enter_context(tc.tile_pool(name="const", bufs=1))
         raw_pool = ctx.enter_context(tc.tile_pool(name="raw", bufs=PREFETCH + 1))
-        grouped_pool = ctx.enter_context(tc.tile_pool(name="grouped", bufs=2 * RUN_PASSES))
+        grouped_pool = ctx.enter_context(tc.tile_pool(name="grouped", bufs=3))
         mx_pool = ctx.enter_context(
-            tc.tile_pool(name="mx", bufs=(LAG_RUNS + 2) * RUN_PASSES)
+            tc.tile_pool(name="mx", bufs=6)
         )
         result_pool = ctx.enter_context(tc.tile_pool(name="result", bufs=ROW_TILES))
         acc_pool = ctx.enter_context(tc.psum_pool(name="acc", bufs=1))
@@ -88,22 +85,23 @@ def tile_switchnet_fstar_pb_k_kernel(tc, h_switch, k2, b2, k3, b3, grad_out, out
         for c in range(CHUNKS):
             chunk_of.extend([(c, local_pass) for local_pass in range(CHUNK_WIDTHS[c])])
 
-        def load_chunk(c):
+        rows_of = {"dy": dy_rows, "k3": k3_rows}
+        raw = {}
+
+        def load_chunk(operand, c):
             first_k = chunk_of.index((c, 0)) * K_PASS
             width = CHUNK_WIDTHS[c] * K_PASS
-            dy_raw = raw_pool.tile([P, ROW_TILES, CHUNK_PASSES * K_PASS], BF16)
-            nc.sync.dma_start(
-                out=dy_raw[:, :, :width], in_=dy_rows[:, :, first_k : first_k + width]
+            raw_tile = raw_pool.tile(
+                [P, ROW_TILES, CHUNK_PASSES * K_PASS], BF16, tag="raw_" + operand
             )
-            k3_raw = raw_pool.tile([P, ROW_TILES, CHUNK_PASSES * K_PASS], BF16)
             nc.sync.dma_start(
-                out=k3_raw[:, :, :width], in_=k3_rows[:, :, first_k : first_k + width]
+                out=raw_tile[:, :, :width], in_=rows_of[operand][:, :, first_k : first_k + width]
             )
-            return dy_raw, k3_raw
+            raw[(operand, c)] = raw_tile
 
-        raw = {}
         for c in range(PREFETCH):
-            raw[c] = load_chunk(c)
+            load_chunk("dy", c)
+            load_chunk("k3", c)
 
         dg_acc = [
             acc_pool.tile([P, ROWS], F32, name="dg_acc%d" % j) for j in range(GROUPS)
@@ -111,53 +109,60 @@ def tile_switchnet_fstar_pb_k_kernel(tc, h_switch, k2, b2, k3, b3, grad_out, out
 
         quantised = {}
 
-        def multiply_run(run):
-            for g in range(run * RUN_PASSES, (run + 1) * RUN_PASSES):
-                dy_codes, dy_scales, k3_codes, k3_scales = quantised[g]
-                for j in range(GROUPS):
-                    group_cols = slice(j * R, (j + 1) * R)
-                    nc.tensor.matmul_mx(
-                        out=dg_acc[j][:],
-                        lhsT=k3_codes[:, group_cols].bitcast(E4M3_X4),
-                        lhsT_scale=k3_scales[:, group_cols],
-                        rhs=dy_codes[:].bitcast(E5M2_X4),
-                        rhs_scale=dy_scales[:],
-                        start=(g == 0),
-                        stop=(g == PASSES - 1),
-                    )
-
-        for run in range(RUNS):
-            run_passes = range(run * RUN_PASSES, (run + 1) * RUN_PASSES)
-            grouped = {}
-            for g in run_passes:
-                c, local_pass = chunk_of[g]
-                if local_pass == 0 and c + PREFETCH < CHUNKS:
-                    raw[c + PREFETCH] = load_chunk(c + PREFETCH)
-                dy_raw, k3_raw = raw[c]
-                dy_grouped = grouped_pool.tile([P, 4 * ROWS], BF16, align_bytes=64)
-                transpose_pass(nc, banks, ident, dy_raw, local_pass, dy_grouped, True)
-                k3_grouped = grouped_pool.tile([P, 4 * ROWS], BF16, align_bytes=64)
-                transpose_pass(
-                    nc, banks, ident, k3_raw, local_pass, k3_grouped, g != run_passes[-1]
+        def multiply_pass(g):
+            dy_codes, dy_scales = quantised[("dy", g)]
+            k3_codes, k3_scales = quantised[("k3", g)]
+            for j in range(GROUPS):
+                group_cols = slice(j * R, (j + 1) * R)
+                nc.tensor.matmul_mx(
+                    out=dg_acc[j][:],
+                    lhsT=k3_codes[:, group_cols].bitcast(E4M3_X4),
+                    lhsT_scale=k3_scales[:, group_cols],
+                    rhs=dy_codes[:].bitcast(E5M2_X4),
+                    rhs_scale=dy_scales[:],
+                    start=(g == 0),
+                    stop=(g == PASSES - 1),
                 )
-                grouped[g] = (dy_grouped, k3_grouped)
 
-            for g in run_passes:
-                dy_grouped, k3_grouped = grouped[g]
-                dy_codes = mx_pool.tile([P, ROWS], U32, align_bytes=64)
-                dy_scales = mx_pool.tile([P, ROWS], U8, align_bytes=64)
-                nc.vector.quantize_mx(
-                    out=dy_codes[:].bitcast(E5M2_X4), scales=dy_scales[:], in_=dy_grouped[:]
-                )
-                k3_codes = mx_pool.tile([P, ROWS], U32, align_bytes=64)
-                k3_scales = mx_pool.tile([P, ROWS], U8, align_bytes=64)
-                nc.vector.quantize_mx(
-                    out=k3_codes[:].bitcast(E4M3_X4), scales=k3_scales[:], in_=k3_grouped[:]
-                )
-                quantised[g] = (dy_codes, dy_scales, k3_codes, k3_scales)
+        x4_of = {"dy": E5M2_X4, "k3": E4M3_X4}
 
-            if run >= LAG_RUNS:
-                multiply_run(run - LAG_RUNS)
+        def transpose_and_quantise(operand, g, vector_helps):
+            c, local_pass = chunk_of[g]
+            if local_pass == 0 and c + PREFETCH < CHUNKS:
+                load_chunk(operand, c + PREFETCH)
+            grouped = grouped_pool.tile(
+                [P, 4 * ROWS], BF16, align_bytes=64, tag="grouped_" + operand
+            )
+            transpose_pass(
+                nc, banks, ident, raw[(operand, c)], local_pass, grouped, vector_helps
+            )
+            codes = mx_pool.tile([P, ROWS], U32, align_bytes=64, tag="codes_" + operand)
+            scales = mx_pool.tile([P, ROWS], U8, align_bytes=64, tag="scales_" + operand)
+            nc.vector.quantize_mx(
+                out=codes[:].bitcast(x4_of[operand]), scales=scales[:], in_=grouped[:]
+            )
+            quantised[(operand, g)] = (codes, scales)
+
+        runs = []
+        for c in range(CHUNKS):
+            first_pass = chunk_of.index((c, 0))
+            if CHUNK_WIDTHS[c] == 1:
+                runs.append([("dy", first_pass), ("k3", first_pass)])
+            else:
+                runs.append([("dy", first_pass), ("dy", first_pass + 1)])
+                runs.append([("k3", first_pass), ("k3", first_pass + 1)])
+
+        completed_in = {}
+        multiplied = 0
+        for r in range(len(runs)):
+            transpose_and_quantise(runs[r][0][0], runs[r][0][1], True)
+            transpose_and_quantise(runs[r][1][0], runs[r][1][1], False)
+            if completed_in.get(multiplied, r) < r:
+                multiply_pass(multiplied)
+                multiplied = multiplied + 1
+            for pair in runs[r]:
+                if pair[0] == "k3":
+                    completed_in[pair[1]] = r
 
         k2_rows = const.tile([P, GROUPS, R], BF16)
         nc.sync.dma_start(out=k2_rows[:], in_=k2.rearrange("j r q -> r j q"))
@@ -167,8 +172,8 @@ def tile_switchnet_fstar_pb_k_kernel(tc, h_switch, k2, b2, k3, b3, grad_out, out
         k2_t = const.tile([P, GROUPS, R], F32)
         nc.scalar.copy(out=k2_t[:], in_=k2_bank[:])
 
-        for run in range(RUNS - LAG_RUNS, RUNS):
-            multiply_run(run)
+        for g in range(multiplied, PASSES):
+            multiply_pass(g)
 
         dg_t = const.tile([P, GROUPS, ROWS], F32)
         for j in range(GROUPS):

@@ -25,6 +25,8 @@ CHUNK_PASSES = 2
 CHUNK_WIDTHS = [CHUNK_PASSES // 2] * 2 + [CHUNK_PASSES] * (PASSES // CHUNK_PASSES - 1)
 CHUNKS = len(CHUNK_WIDTHS)
 PREFETCH = 4
+WARM_UP_MATMULS = 5
+LAST_TOGETHER = 2
 
 FLOPS = 2 * ROWS * ROWS * WINDOW + 2 * ROWS * GROUPS * R * R
 
@@ -61,7 +63,7 @@ def tile_switchnet_fstar_pb_k_kernel(tc, h_switch, k2, b2, k3, b3, grad_out, out
     nc = tc.nc
     dy_rows = grad_out.rearrange("(t p) x y c -> p t (x y c)", p=P)
     k3_rows = k3[0].rearrange("(t p) l -> p t l", p=P)
-    out_rows = out.rearrange("(t p) j r -> t p (j r)", p=P)
+    out_groups = out.rearrange("(t p) j r -> j p t r", p=P)
 
     with ExitStack() as ctx:
         const = ctx.enter_context(tc.tile_pool(name="const", bufs=1))
@@ -70,7 +72,7 @@ def tile_switchnet_fstar_pb_k_kernel(tc, h_switch, k2, b2, k3, b3, grad_out, out
         mx_pool = ctx.enter_context(
             tc.tile_pool(name="mx", bufs=6)
         )
-        result_pool = ctx.enter_context(tc.tile_pool(name="result", bufs=ROW_TILES))
+        result_pool = ctx.enter_context(tc.tile_pool(name="result", bufs=2 * GROUPS))
         acc_pool = ctx.enter_context(tc.psum_pool(name="acc", bufs=1))
         banks = ctx.enter_context(tc.psum_pool(name="banks", bufs=4))
 
@@ -103,26 +105,37 @@ def tile_switchnet_fstar_pb_k_kernel(tc, h_switch, k2, b2, k3, b3, grad_out, out
             load_chunk("dy", c)
             load_chunk("k3", c)
 
+        zeros = const.tile([P, BANK], BF16)
+        nc.vector.memset(zeros[:], 0.0)
+        warm_bank = banks.tile([P, BANK], F32, tag="bank")
+        for i in range(WARM_UP_MATMULS):
+            nc.tensor.matmul(
+                out=warm_bank[:], lhsT=zeros[:, :P], rhs=zeros[:], start=True, stop=True
+            )
+
         dg_acc = [
             acc_pool.tile([P, ROWS], F32, name="dg_acc%d" % j) for j in range(GROUPS)
         ]
 
         quantised = {}
 
-        def multiply_pass(g):
+        def multiply_group(g, j):
             dy_codes, dy_scales = quantised[("dy", g)]
             k3_codes, k3_scales = quantised[("k3", g)]
+            group_cols = slice(j * R, (j + 1) * R)
+            nc.tensor.matmul_mx(
+                out=dg_acc[j][:],
+                lhsT=k3_codes[:, group_cols].bitcast(E4M3_X4),
+                lhsT_scale=k3_scales[:, group_cols],
+                rhs=dy_codes[:].bitcast(E5M2_X4),
+                rhs_scale=dy_scales[:],
+                start=(g == 0),
+                stop=(g == PASSES - 1),
+            )
+
+        def multiply_pass(g):
             for j in range(GROUPS):
-                group_cols = slice(j * R, (j + 1) * R)
-                nc.tensor.matmul_mx(
-                    out=dg_acc[j][:],
-                    lhsT=k3_codes[:, group_cols].bitcast(E4M3_X4),
-                    lhsT_scale=k3_scales[:, group_cols],
-                    rhs=dy_codes[:].bitcast(E5M2_X4),
-                    rhs_scale=dy_scales[:],
-                    start=(g == 0),
-                    stop=(g == PASSES - 1),
-                )
+                multiply_group(g, j)
 
         x4_of = {"dy": E5M2_X4, "k3": E4M3_X4}
 
@@ -172,8 +185,11 @@ def tile_switchnet_fstar_pb_k_kernel(tc, h_switch, k2, b2, k3, b3, grad_out, out
         k2_t = const.tile([P, GROUPS, R], F32)
         nc.scalar.copy(out=k2_t[:], in_=k2_bank[:])
 
-        for g in range(multiplied, PASSES):
+        for g in range(multiplied, PASSES - LAST_TOGETHER):
             multiply_pass(g)
+        for j in range(GROUPS):
+            for g in range(PASSES - LAST_TOGETHER, PASSES):
+                multiply_group(g, j)
 
         dg_t = const.tile([P, GROUPS, ROWS], F32)
         for j in range(GROUPS):
@@ -182,19 +198,21 @@ def tile_switchnet_fstar_pb_k_kernel(tc, h_switch, k2, b2, k3, b3, grad_out, out
             else:
                 nc.vector.tensor_copy(out=dg_t[:, j, :], in_=dg_acc[j][:])
 
-        for t in range(ROW_TILES):
-            out_bank = banks.tile([P, GROUPS, R], F32, tag="bank")
-            for j in range(GROUPS):
-                nc.tensor.matmul(
-                    out=out_bank[:, j, :],
-                    lhsT=dg_t[:, j, t * P : (t + 1) * P],
-                    rhs=k2_t[:, j, :],
-                    start=True,
-                    stop=True,
-                )
-            result = result_pool.tile([P, GROUPS, R], F32)
-            if t % 2 == 0:
-                nc.scalar.copy(out=result[:], in_=out_bank[:])
-            else:
-                nc.vector.tensor_copy(out=result[:], in_=out_bank[:])
-            nc.sync.dma_start(out=out_rows[t], in_=result[:].rearrange("p j r -> p (j r)"))
+        for j in range(GROUPS):
+            for half in range(2):
+                out_bank = banks.tile([P, 2, R], F32, tag="bank")
+                for i in range(2):
+                    t = 2 * half + i
+                    nc.tensor.matmul(
+                        out=out_bank[:, i, :],
+                        lhsT=dg_t[:, j, t * P : (t + 1) * P],
+                        rhs=k2_t[:, j, :],
+                        start=True,
+                        stop=True,
+                    )
+                result = result_pool.tile([P, 2, R], F32)
+                if half == 0:
+                    nc.scalar.copy(out=result[:], in_=out_bank[:])
+                else:
+                    nc.vector.tensor_copy(out=result[:], in_=out_bank[:])
+                nc.sync.dma_start(out=out_groups[j][:, 2 * half : 2 * half + 2, :], in_=result[:])

@@ -105,14 +105,6 @@ def tile_switchnet_fstar_pb_k_kernel(tc, h_switch, k2, b2, k3, b3, grad_out, out
             load_chunk("dy", c)
             load_chunk("k3", c)
 
-        zeros = const.tile([P, BANK], BF16)
-        nc.vector.memset(zeros[:], 0.0)
-        warm_bank = banks.tile([P, BANK], F32, tag="bank")
-        for i in range(WARM_UP_MATMULS):
-            nc.tensor.matmul(
-                out=warm_bank[:], lhsT=zeros[:, :P], rhs=zeros[:], start=True, stop=True
-            )
-
         dg_acc = [
             acc_pool.tile([P, ROWS], F32, name="dg_acc%d" % j) for j in range(GROUPS)
         ]

@@ -25,7 +25,6 @@ CHUNK_PASSES = 2
 CHUNK_WIDTHS = [CHUNK_PASSES // 2] * 2 + [CHUNK_PASSES] * (PASSES // CHUNK_PASSES - 1)
 CHUNKS = len(CHUNK_WIDTHS)
 PREFETCH = 4
-WARM_UP_MATMULS = 5
 LAST_TOGETHER = 2
 
 FLOPS = 2 * ROWS * ROWS * WINDOW + 2 * ROWS * GROUPS * R * R
@@ -143,9 +142,15 @@ def tile_switchnet_fstar_pb_k_kernel(tc, h_switch, k2, b2, k3, b3, grad_out, out
             )
             codes = mx_pool.tile([P, ROWS], U32, align_bytes=64, tag="codes_" + operand)
             scales = mx_pool.tile([P, ROWS], U8, align_bytes=64, tag="scales_" + operand)
-            nc.vector.quantize_mx(
-                out=codes[:].bitcast(x4_of[operand]), scales=scales[:], in_=grouped[:]
-            )
+            pieces = 2 if operand == "k3" else 1
+            piece_rows = ROWS // pieces
+            for piece in range(pieces):
+                piece_cols = slice(piece * piece_rows, (piece + 1) * piece_rows)
+                nc.vector.quantize_mx(
+                    out=codes[:, piece_cols].bitcast(x4_of[operand]),
+                    scales=scales[:, piece_cols],
+                    in_=grouped[:, 4 * piece * piece_rows : 4 * (piece + 1) * piece_rows],
+                )
             quantised[(operand, g)] = (codes, scales)
 
         runs = []

from contextlib import ExitStack

import concourse.mybir as mybir
from concourse.masks import make_identity

F32 = mybir.dt.float32
BF16 = mybir.dt.bfloat16
U32 = mybir.dt.uint32
U8 = mybir.dt.uint8
E4M3_X4 = mybir.dt.float8_e4m3fn_x4
E5M2_X4 = mybir.dt.float8_e5m2_x4

P = 128
ROWS = 512
ROW_TILES = ROWS // P
WINDOW = 16384
GROUPS = 4
R = 128
K_PASS = 4 * P
PASSES = WINDOW // K_PASS
WORDS = K_PASS // 2
BANK = 512

CHUNK_PASSES = 2
CHUNK_WIDTHS = [CHUNK_PASSES // 2] * 2 + [CHUNK_PASSES] * (PASSES // CHUNK_PASSES - 1)
CHUNKS = len(CHUNK_WIDTHS)
PREFETCH = 4
LAST_TOGETHER = 2

FLOPS = 2 * ROWS * ROWS * WINDOW + 2 * ROWS * GROUPS * R * R


def transpose_pass(nc, banks, ident, raw, local_pass, grouped, vector_helps):
    raw_words = raw[:].bitcast(F32)
    grouped_words = grouped[:].bitcast(F32)
    first_word = local_pass * WORDS
    tiles_per_bank = BANK // (2 * P)
    for half in range(ROW_TILES // tiles_per_bank):
        bank = banks.tile([P, 2, tiles_per_bank * P], F32, tag="bank")
        for u in range(2):
            for i in range(tiles_per_bank):
                nc.tensor.transpose(
                    bank[:, u, i * P : (i + 1) * P],
                    raw_words[
                        :,
                        half * tiles_per_bank + i,
                        first_word + u * P : first_word + (u + 1) * P,
                    ],
                    ident[:],
                )
        src = bank[:].rearrange("p u c -> p c u")
        dst = grouped_words[:, half * BANK : (half + 1) * BANK].rearrange(
            "p (c u) -> p c u", u=2
        )
        if vector_helps and half == 1:
            nc.vector.tensor_copy(out=dst, in_=src)
        else:
            nc.scalar.copy(out=dst, in_=src)


def tile_switchnet_fstar_pb_k_kernel(tc, h_switch, k2, b2, k3, b3, grad_out, out):
    nc = tc.nc
    dy_rows = grad_out.rearrange("(t p) x y c -> p t (x y c)", p=P)
    k3_rows = k3[0].rearrange("(t p) l -> p t l", p=P)
    out_groups = out.rearrange("(t p) j r -> j p t r", p=P)

    with ExitStack() as ctx:
        const = ctx.enter_context(tc.tile_pool(name="const", bufs=1))
        raw_pool = ctx.enter_context(tc.tile_pool(name="raw", bufs=PREFETCH + 1))
        grouped_pool = ctx.enter_context(tc.tile_pool(name="grouped", bufs=3))
        mx_pool = ctx.enter_context(
            tc.tile_pool(name="mx", bufs=6)
        )
        result_pool = ctx.enter_context(tc.tile_pool(name="result", bufs=2 * GROUPS))
        acc_pool = ctx.enter_context(tc.psum_pool(name="acc", bufs=1))
        banks = ctx.enter_context(tc.psum_pool(name="banks", bufs=4))

        ident = const.tile([P, P], F32)
        make_identity(nc, ident[:])
        ident_bf16 = const.tile([P, P], BF16)
        make_identity(nc, ident_bf16[:])

        ctx.enter_context(tc.manual_schedule())

        chunk_of = []
        for c in range(CHUNKS):
            chunk_of.extend([(c, local_pass) for local_pass in range(CHUNK_WIDTHS[c])])

        rows_of = {"dy": dy_rows, "k3": k3_rows}
        raw = {}

        def load_chunk(operand, c):
            first_k = chunk_of.index((c, 0)) * K_PASS
            width = CHUNK_WIDTHS[c] * K_PASS
            raw_tile = raw_pool.tile(
                [P, ROW_TILES, CHUNK_PASSES * K_PASS], BF16, tag="raw_" + operand
            )
            nc.sync.dma_start(
                out=raw_tile[:, :, :width], in_=rows_of[operand][:, :, first_k : first_k + width]
            )
            raw[(operand, c)] = raw_tile

        for c in range(PREFETCH):
            load_chunk("dy", c)
            load_chunk("k3", c)

        dg_acc = [
            acc_pool.tile([P, ROWS], F32, name="dg_acc%d" % j) for j in range(GROUPS)
        ]

        quantised = {}

        def multiply_group(g, j):
            dy_codes, dy_scales = quantised[("dy", g)]
            k3_codes, k3_scales = quantised[("k3", g)]
            group_cols = slice(j * R, (j + 1) * R)
            nc.tensor.matmul_mx(
                out=dg_acc[j][:],
                lhsT=k3_codes[:, group_cols].bitcast(E4M3_X4),
                lhsT_scale=k3_scales[:, group_cols],
                rhs=dy_codes[:].bitcast(E5M2_X4),
                rhs_scale=dy_scales[:],
                start=(g == 0),
                stop=(g == PASSES - 1),
            )

        def multiply_pass(g):
            for j in range(GROUPS):
                multiply_group(g, j)

        x4_of = {"dy": E5M2_X4, "k3": E4M3_X4}

        def transpose_and_quantise(operand, g, vector_helps):
            c, local_pass = chunk_of[g]
            if local_pass == 0 and c + PREFETCH < CHUNKS:
                load_chunk(operand, c + PREFETCH)
            grouped = grouped_pool.tile(
                [P, 4 * ROWS], BF16, align_bytes=64, tag="grouped_" + operand
            )
            transpose_pass(
                nc, banks, ident, raw[(operand, c)], local_pass, grouped, vector_helps
            )
            codes = mx_pool.tile([P, ROWS], U32, align_bytes=64, tag="codes_" + operand)
            scales = mx_pool.tile([P, ROWS], U8, align_bytes=64, tag="scales_" + operand)
            pieces = 2 if operand == "k3" else 1
            piece_rows = ROWS // pieces
            for piece in range(pieces):
                piece_cols = slice(piece * piece_rows, (piece + 1) * piece_rows)
                nc.vector.quantize_mx(
                    out=codes[:, piece_cols].bitcast(x4_of[operand]),
                    scales=scales[:, piece_cols],
                    in_=grouped[:, 4 * piece * piece_rows : 4 * (piece + 1) * piece_rows],
                )
            quantised[(operand, g)] = (codes, scales)

        runs = []
        for c in range(CHUNKS):
            first_pass = chunk_of.index((c, 0))
            if CHUNK_WIDTHS[c] == 1:
                runs.append([("dy", first_pass), ("k3", first_pass)])
            else:
                runs.append([("dy", first_pass), ("dy", first_pass + 1)])
                runs.append([("k3", first_pass), ("k3", first_pass + 1)])

        completed_in = {}
        multiplied = 0
        for r in range(len(runs)):
            transpose_and_quantise(runs[r][0][0], runs[r][0][1], True)
            transpose_and_quantise(runs[r][1][0], runs[r][1][1], False)
            if completed_in.get(multiplied, r) < r:
                multiply_pass(multiplied)
                multiplied = multiplied + 1
            for pair in runs[r]:
                if pair[0] == "k3":
                    completed_in[pair[1]] = r

        k2_rows = const.tile([P, GROUPS, R], BF16)
        nc.sync.dma_start(out=k2_rows[:], in_=k2.rearrange("j r q -> r j q"))
        k2_bank = banks.tile([P, GROUPS, R], BF16, tag="bank")
        for j in range(GROUPS):
            nc.tensor.transpose(k2_bank[:, j, :], k2_rows[:, j, :], ident_bf16[:])
        k2_t = const.tile([P, GROUPS, R], F32)
        nc.scalar.copy(out=k2_t[:], in_=k2_bank[:])

        for g in range(multiplied, PASSES - LAST_TOGETHER):
            multiply_pass(g)
        for j in range(GROUPS):
            for g in range(PASSES - LAST_TOGETHER, PASSES):
                multiply_group(g, j)

        dg_t = const.tile([P, GROUPS, ROWS], F32)
        for j in range(GROUPS):
            if j % 2 == 0:
                nc.scalar.copy(out=dg_t[:, j, :], in_=dg_acc[j][:])
            else:
                nc.vector.tensor_copy(out=dg_t[:, j, :], in_=dg_acc[j][:])

        for j in range(GROUPS):
            for half in range(2):
                out_bank = banks.tile([P, 2, R], F32, tag="bank")
                for i in range(2):
                    t = 2 * half + i
                    nc.tensor.matmul(
                        out=out_bank[:, i, :],
                        lhsT=dg_t[:, j, t * P : (t + 1) * P],
                        rhs=k2_t[:, j, :],
                        start=True,
                        stop=True,
                    )
                result = result_pool.tile([P, 2, R], F32)
                if half == 0:
                    nc.scalar.copy(out=result[:], in_=out_bank[:])
                else:
                    nc.vector.tensor_copy(out=result[:], in_=out_bank[:])
                nc.sync.dma_start(out=out_groups[j][:, 2 * half : 2 * half + 2, :], in_=result[:])
